import numpy as np
import ml_dtypes


def mxq(x, axis, fmt="e4m3"):
    dtype, down = {"e4m3": (ml_dtypes.float8_e4m3fn, 7), "e5m2": (ml_dtypes.float8_e5m2, 14)}[fmt]
    v = np.moveaxis(np.asarray(x, np.float32).astype(ml_dtypes.bfloat16).astype(np.float64), axis, -1)
    blocks = v.reshape(v.shape[:-1] + (-1, 32))
    amax = np.abs(blocks).max(-1, keepdims=True)
    byte = np.maximum(np.where(amax > 0, np.frexp(amax)[1] - 1 + 127, 0) - down, 1)
    scale = np.exp2(byte - 127.0)
    codes = (blocks / scale).astype(np.float32).astype(dtype).astype(np.float64)
    return np.moveaxis((codes * scale).reshape(v.shape), -1, axis)


WIDE = False


def mx_kscale(k):
    if not WIDE:
        return np.ones(k)
    levels = np.array([10, -10, 5, -5, 0])
    a = np.random.permutation(np.resize(levels, k // 512 * 4)).reshape(k // 512, 4)
    idx = np.arange(k)
    return np.exp2(a[idx // 512, idx % 128 // 32])


BF16 = ml_dtypes.bfloat16


def bf(x):
    return np.asarray(x, np.float32).astype(BF16)


def f64(x):
    return np.asarray(x).astype(np.float64)


B, N, NI, NH, NO = 2, 256, 128, 512, 4
CONTEXT = 3
H = NH * CONTEXT


def _shift(x, d):
    if d == 0:
        return x
    if d > 0:
        return np.pad(x[:, d:, :], ((0, 0), (0, d), (0, 0)))
    return np.pad(x[:, :d, :], ((0, 0), (-d, 0), (0, 0)))


def setup_inputs():
    u = mx_kscale(NH)
    uu = np.tile(u, CONTEXT)
    return {"x": bf(np.random.standard_normal((B, N, NI))),
            "W_lin": bf(np.random.standard_normal((NI, NH)) / np.sqrt(NI) * u),
            "b_lin": bf(np.random.standard_normal(NH) * 0.3 * u),
            "W_bil": bf(np.random.standard_normal((NO, H, H)) * 8.0 / H / uu[:, None] / uu[None, :]),
            "b_bil": bf(np.random.standard_normal(NO))}


def reference(x, W_lin, b_lin, W_bil, b_bil):
    h = np.maximum(f64(x) @ f64(W_lin) + f64(b_lin), 0.0)
    hq = mxq(h, 2, "e4m3")
    w = CONTEXT // 2
    wr = f64(W_bil).reshape(NO, CONTEXT, NH, H).transpose(2, 1, 0, 3).reshape(NH, CONTEXT * NO * H)
    p = (hq @ mxq(wr, 0, "e4m3")).reshape(B, N, CONTEXT, NO * H)
    t = sum(_shift(p[:, :, c, :], c - w) for c in range(CONTEXT))
    tr = t.reshape(B, N * NO * CONTEXT, NH).transpose(0, 2, 1)
    q = (hq @ mxq(tr, 1, "e4m3")).reshape(B, N, N * NO, CONTEXT)
    o = sum(_shift(q[:, :, :, c], c - w) for c in range(CONTEXT))
    return o.reshape(B, N, N, NO).transpose(0, 2, 1, 3) + f64(b_bil)

@@ -1,0 +1,228 @@
+from contextlib import ExitStack
+
+import concourse.mybir as mybir
+from concourse.masks import make_identity
+
+BF16 = mybir.dt.bfloat16
+F32 = mybir.dt.float32
+U32 = mybir.dt.uint32
+U8 = mybir.dt.uint8
+FP8X4 = mybir.dt.float8_e4m3fn_x4
+ACT = mybir.ActivationFunctionType
+ALU = mybir.AluOpType
+
+P = 128
+B, N, NI, NH, NO = 2, 256, 128, 512, 4
+CTX = 3
+H = NH * CTX
+TOK = B * N
+FLOPS = 2 * TOK * NI * NH + 2 * TOK * H * NO * H + 2 * B * N * NO * N * H
+PIN = True
+RAW_BUFS = 6
+SCALAR_EXTRA = ((1, 1),)
+
+
+def regroup_views(dst, src):
+    return (
+        dst.rearrange("p (c i) t -> p c t i", i=4),
+        src.rearrange("p t (c i) -> p c t i", i=4),
+    )
+
+
+def tile_bilinearpairedlayer_kernel(tc, x, W_lin, b_lin, W_bil, b_bil, out):
+    nc = tc.nc
+    with ExitStack() as ctx:
+        if PIN:
+            ctx.enter_context(tc.manual_schedule())
+        const = ctx.enter_context(tc.tile_pool(name="const", bufs=1))
+        rawp = ctx.enter_context(tc.tile_pool(name="rawp", bufs=RAW_BUFS))
+        grpp = ctx.enter_context(tc.tile_pool(name="grpp", bufs=6))
+        wcp = ctx.enter_context(tc.tile_pool(name="wcp", bufs=3))
+        gtp = ctx.enter_context(tc.tile_pool(name="gtp", bufs=3))
+        resp = ctx.enter_context(tc.tile_pool(name="resp", bufs=4))
+        psum = ctx.enter_context(tc.psum_pool(name="psum", bufs=8))
+
+        x_sb = const.tile([P, 4, NI], BF16)
+        nc.sync.dma_start(out=x_sb[:], in_=x.flatten_outer_dims().rearrange("(a p) n -> p a n", p=P))
+        wl = const.tile([P, NH], BF16)
+        nc.sync.dma_start(out=wl[:], in_=W_lin)
+        blr = const.tile([P, P], BF16)
+        nc.vector.memset(blr[:], 0.0)
+        nc.sync.dma_start(out=blr[0:4, :], in_=b_lin.rearrange("(j p) -> j p", p=P))
+        bb = const.tile([P, NO], BF16)
+        nc.scalar.dma_start(out=bb[:], in_=b_bil.partition_broadcast(P))
+
+        raw = {}
+
+        def load(o, c, lo, hi):
+            if (o, c) not in raw:
+                raw[(o, c)] = rawp.tile([P, 4, H], BF16, tag="raw", name="raw_%d_%d" % (o, c))
+            src = W_bil[o, c * NH:(c + 1) * NH, lo:hi].rearrange("(j p) g -> p j g", p=P)
+            nc.sync.dma_start(out=raw[(o, c)][:, :, lo:hi], in_=src)
+
+        for c in range(CTX):
+            load(0, c, 0, NH)
+        for c in range(CTX):
+            load(0, c, NH, H)
+        for c in range(CTX):
+            load(1, c, 0, H)
+
+        ident = const.tile([P, P], BF16)
+        make_identity(nc, ident[:])
+
+        hg = [const.tile([P, TOK, 4], BF16, align_bytes=64, name="hg%d" % c) for c in range(CTX)]
+        hv = [hg[c][:].rearrange("p (b i) t -> p b (i t)", b=B) for c in range(CTX)]
+        nc.vector.memset(hv[0][:, :, 0:4], 0.0)
+        nc.vector.memset(hv[2][:, :, 4 * N - 4:4 * N], 0.0)
+
+        units = [(o, g) for o in range(NO) for g in range(CTX)]
+        wcs = {}
+
+        def prep_copies(u):
+            o, g = units[u]
+            grs = []
+            for c in (2, 0, 1):
+                gr = grpp.tile([P, NH, 4], BF16, align_bytes=64, tag="grp", name="grp_%d_%d" % (u, c))
+                dst, src = regroup_views(gr[:], raw[(o, c)][:, :, g * NH:(g + 1) * NH])
+                if (u, c) in SCALAR_EXTRA or c == 2:
+                    nc.scalar.copy(out=dst, in_=src)
+                else:
+                    nc.vector.tensor_copy(out=dst, in_=src)
+                grs.append((c, gr))
+            return grs
+
+        def prep_quant(u, grs, which):
+            if u not in wcs:
+                wc = wcp.tile([P, CTX, NH], U32, align_bytes=64, tag="wc", name="wc_%d" % u)
+                ws = wcp.tile([P, CTX, NH], U8, align_bytes=64, tag="ws", name="ws_%d" % u)
+                wcs[u] = (wc, ws)
+            wc, ws = wcs[u]
+            for c, gr in sorted(grs, key=lambda e: e[0]):
+                if c in which:
+                    nc.vector.quantize_mx(
+                        out=wc[:, c, :].bitcast(FP8X4),
+                        scales=ws[:, c, :],
+                        in_=gr[:].rearrange("p w t -> p (w t)"),
+                    )
+
+        tp = psum.tile([P, 5, P], BF16, tag="bank", name="tp")
+        for a in range(4):
+            nc.tensor.transpose(tp[:, a, :], x_sb[:, a, :], ident[:])
+        nc.tensor.transpose(tp[:, 4, :], blr[:], ident[:])
+        xT = const.tile([P, TOK], BF16)
+        nc.vector.tensor_copy(out=xT[:], in_=tp[:, 0:4, :].rearrange("p a t -> p (a t)"))
+        blf = const.tile([P, 4], F32)
+        nc.vector.tensor_copy(out=blf[:], in_=tp[:, 4, 0:4])
+
+        hpl = const.tile([P, 4, TOK], BF16)
+        for j in range(4):
+            hp = psum.tile([P, TOK], F32, tag="bank", name="hp%d" % j)
+            nc.tensor.matmul(hp[:], lhsT=wl[:, j * P:(j + 1) * P], rhs=xT[:], start=True, stop=True)
+            nc.scalar.activation(out=hpl[:, j, :], in_=hp[:], func=ACT.Relu, bias=blf[:, j:j + 1], scale=1.0)
+
+        grs0 = prep_copies(0)
+        prep_quant(0, grs0, (0, 1))
+
+        dst, src = regroup_views(hg[1][:], hpl[:])
+        nc.vector.tensor_copy(out=dst, in_=src)
+        nc.vector.tensor_copy(out=hv[0][:, :, 4:4 * N], in_=hv[1][:, :, 0:4 * N - 4])
+        nc.vector.tensor_copy(out=hv[2][:, :, 0:4 * N - 4], in_=hv[1][:, :, 4:4 * N])
+        hc = const.tile([P, CTX, TOK], U32, align_bytes=64)
+        hs = const.tile([P, CTX, TOK], U8, align_bytes=64)
+        for c in (1, 0, 2):
+            nc.vector.quantize_mx(
+                out=hc[:, c, :].bitcast(FP8X4),
+                scales=hs[:, c, :],
+                in_=hg[c][:].rearrange("p w t -> p (w t)"),
+            )
+        prep_quant(0, grs0, (2,))
+
+        tcq = const.tile([P, NO * CTX, TOK], U32, align_bytes=64)
+        tsq = const.tile([P, NO * CTX, TOK], U8, align_bytes=64)
+        gts = {}
+
+        def stage2(u):
+            wc, ws = wcs[u]
+            gt = gtp.tile([P, 4, P, 4], BF16, align_bytes=64, tag="gt", name="gt_%d" % u)
+            gts[u] = gt
+            for r in range(4):
+                bank = psum.tile([P, 4, P], F32, tag="bank", name="t_%d_%d" % (u, r))
+                for tt in range(4):
+                    for c in range(CTX):
+                        nc.tensor.matmul_mx(
+                            out=bank[:, tt, :],
+                            lhsT=wc[:, c, tt * P:(tt + 1) * P].bitcast(FP8X4),
+                            lhsT_scale=ws[:, c, tt * P:(tt + 1) * P],
+                            rhs=hc[:, c, r * P:(r + 1) * P].bitcast(FP8X4),
+                            rhs_scale=hs[:, c, r * P:(r + 1) * P],
+                            start=(c == 0),
+                            stop=(c == CTX - 1),
+                        )
+                if u == len(units) - 1 and r % 2 == 1:
+                    nc.vector.tensor_copy(out=gt[:, r, :, :], in_=bank[:].rearrange("p t r -> p r t"))
+                else:
+                    nc.scalar.copy(out=gt[:, r, :, :], in_=bank[:].rearrange("p t r -> p r t"))
+
+        def quant_t(u):
+            nc.vector.quantize_mx(
+                out=tcq[:, u, :].bitcast(FP8X4),
+                scales=tsq[:, u, :],
+                in_=gts[u][:].rearrange("p r w t -> p (r w t)"),
+            )
+
+        n_units = len(units)
+        for u in range(n_units):
+            if u + 1 < n_units:
+                prep_quant(u + 1, prep_copies(u + 1), (0, 1, 2))
+                o1, g1 = units[u + 1]
+                if g1 == CTX - 1 and o1 + 2 < NO:
+                    for c in range(CTX):
+                        load(o1 + 2, c, 0, H)
+            if u == n_units - 1:
+                quant_t(u - 1)
+                stage2(u)
+            else:
+                stage2(u)
+                if u >= 1:
+                    quant_t(u - 1)
+        bias_t = const.tile([P, P, NO], F32)
+        nc.vector.tensor_copy(out=bias_t[:], in_=bb[:].unsqueeze(1).to_broadcast([P, P, NO]))
+        quant_t(n_units - 1)
+
+        blocks = [(b, it, jh) for b in range(B) for it in range(2) for jh in range(2)]
+        obank = {}
+
+        def stage3(k, us):
+            b, it, jh = blocks[k]
+            if k not in obank:
+                obank[k] = psum.tile([P, NO, P], F32, tag="bank", name="o_%d" % k)
+            ti = b * N + it * P
+            tj = b * N + jh * P
+            for u in us:
+                o, g = units[u]
+                nc.tensor.matmul_mx(
+                    out=obank[k][:, o, :],
+                    lhsT=tcq[:, u, ti:ti + P].bitcast(FP8X4),
+                    lhsT_scale=tsq[:, u, ti:ti + P],
+                    rhs=hc[:, g, tj:tj + P].bitcast(FP8X4),
+                    rhs_scale=hs[:, g, tj:tj + P],
+                    start=(g == 0),
+                    stop=(g == CTX - 1),
+                )
+
+        def finish(k):
+            b, it, jh = blocks[k]
+            res = resp.tile([P, P, NO], F32, tag="res", name="res_%d" % k)
+            nc.vector.tensor_tensor(
+                out=res[:], in0=obank[k][:].rearrange("p o j -> p j o"), in1=bias_t[:], op=ALU.add
+            )
+            nc.sync.dma_start(out=out[b, it * P:(it + 1) * P, jh * P:(jh + 1) * P, :], in_=res[:])
+
+        for k in range(4):
+            stage3(k, range(n_units - 1))
+        for k in range(4):
+            stage3(k, [n_units - 1])
+            finish(k)
+        for k in range(4, 8):
+            stage3(k, range(n_units))
+            finish(k)

@@ -18,8 +18,7 @@ H = NH * CTX
 TOK = B * N
 FLOPS = 2 * TOK * NI * NH + 2 * TOK * H * NO * H + 2 * B * N * NO * N * H
 PIN = True
-RAW_BUFS = 6
-SCALAR_EXTRA = ((1, 1),)
+RAW_UNITS = 7
 
 
 def regroup_views(dst, src):
@@ -35,12 +34,15 @@ def tile_bilinearpairedlayer_kernel(tc, x, W_lin, b_lin, W_bil, b_bil, out):
         if PIN:
             ctx.enter_context(tc.manual_schedule())
         const = ctx.enter_context(tc.tile_pool(name="const", bufs=1))
-        rawp = ctx.enter_context(tc.tile_pool(name="rawp", bufs=RAW_BUFS))
-        grpp = ctx.enter_context(tc.tile_pool(name="grpp", bufs=6))
+        rawp = ctx.enter_context(tc.tile_pool(name="rawp", bufs=CTX * RAW_UNITS))
+        grpp = ctx.enter_context(tc.tile_pool(name="grpp", bufs=2))
         wcp = ctx.enter_context(tc.tile_pool(name="wcp", bufs=3))
         gtp = ctx.enter_context(tc.tile_pool(name="gtp", bufs=3))
         resp = ctx.enter_context(tc.tile_pool(name="resp", bufs=4))
-        psum = ctx.enter_context(tc.psum_pool(name="psum", bufs=8))
+        psum = ctx.enter_context(tc.psum_pool(name="psum", bufs=4))
+
+        units = [(o, g) for o in range(NO) for g in range(CTX)]
+        n_units = len(units)
 
         x_sb = const.tile([P, 4, NI], BF16)
         nc.sync.dma_start(out=x_sb[:], in_=x.flatten_outer_dims().rearrange("(a p) n -> p a n", p=P))
@@ -54,18 +56,15 @@ def tile_bilinearpairedlayer_kernel(tc, x, W_lin, b_lin, W_bil, b_bil, out):
 
         raw = {}
 
-        def load(o, c, lo, hi):
-            if (o, c) not in raw:
-                raw[(o, c)] = rawp.tile([P, 4, H], BF16, tag="raw", name="raw_%d_%d" % (o, c))
-            src = W_bil[o, c * NH:(c + 1) * NH, lo:hi].rearrange("(j p) g -> p j g", p=P)
-            nc.sync.dma_start(out=raw[(o, c)][:, :, lo:hi], in_=src)
+        def load(u):
+            o, g = units[u]
+            for c in range(CTX):
+                raw[(u, c)] = rawp.tile([P, 4, NH], BF16, tag="raw", name="raw_%d_%d" % (u, c))
+                src = W_bil[o, c * NH:(c + 1) * NH, g * NH:(g + 1) * NH]
+                nc.sync.dma_start(out=raw[(u, c)][:], in_=src.rearrange("(j p) g -> p j g", p=P))
 
-        for c in range(CTX):
-            load(0, c, 0, NH)
-        for c in range(CTX):
-            load(0, c, NH, H)
-        for c in range(CTX):
-            load(1, c, 0, H)
+        for u in range(RAW_UNITS):
+            load(u)
 
         ident = const.tile([P, P], BF16)
         make_identity(nc, ident[:])
@@ -75,37 +74,41 @@ def tile_bilinearpairedlayer_kernel(tc, x, W_lin, b_lin, W_bil, b_bil, out):
         nc.vector.memset(hv[0][:, :, 0:4], 0.0)
         nc.vector.memset(hv[2][:, :, 4 * N - 4:4 * N], 0.0)
 
-        units = [(o, g) for o in range(NO) for g in range(CTX)]
+        grs = {}
         wcs = {}
 
         def prep_copies(u):
-            o, g = units[u]
-            grs = []
-            for c in (2, 0, 1):
-                gr = grpp.tile([P, NH, 4], BF16, align_bytes=64, tag="grp", name="grp_%d_%d" % (u, c))
-                dst, src = regroup_views(gr[:], raw[(o, c)][:, :, g * NH:(g + 1) * NH])
-                if (u, c) in SCALAR_EXTRA or c == 2:
-                    nc.scalar.copy(out=dst, in_=src)
-                else:
-                    nc.vector.tensor_copy(out=dst, in_=src)
-                grs.append((c, gr))
-            return grs
+            g2 = grpp.tile([P, NH, 4], BF16, align_bytes=64, tag="grp2", name="grp2_%d" % u)
+            dst, src = regroup_views(g2[:], raw[(u, 2)][:])
+            nc.scalar.copy(out=dst, in_=src)
+            g01 = grpp.tile([P, 2, NH, 4], BF16, align_bytes=64, tag="grp01", name="grp01_%d" % u)
+            for c in range(2):
+                dst, src = regroup_views(g01[:, c, :, :], raw[(u, c)][:])
+                nc.vector.tensor_copy(out=dst, in_=src)
+            grs[u] = (g01, g2)
+            wc = wcp.tile([P, CTX, NH], U32, align_bytes=64, tag="wc", name="wc_%d" % u)
+            ws = wcp.tile([P, CTX, NH], U8, align_bytes=64, tag="ws", name="ws_%d" % u)
+            wcs[u] = (wc, ws)
+            if u + RAW_UNITS < n_units:
+                load(u + RAW_UNITS)
 
-        def prep_quant(u, grs, which):
-            if u not in wcs:
-                wc = wcp.tile([P, CTX, NH], U32, align_bytes=64, tag="wc", name="wc_%d" % u)
-                ws = wcp.tile([P, CTX, NH], U8, align_bytes=64, tag="ws", name="ws_%d" % u)
-                wcs[u] = (wc, ws)
+        def prep_quant01(u):
             wc, ws = wcs[u]
-            for c, gr in sorted(grs, key=lambda e: e[0]):
-                if c in which:
-                    nc.vector.quantize_mx(
-                        out=wc[:, c, :].bitcast(FP8X4),
-                        scales=ws[:, c, :],
-                        in_=gr[:].rearrange("p w t -> p (w t)"),
-                    )
+            nc.vector.quantize_mx(
+                out=wc[:, 0:2, :].rearrange("p c w -> p (c w)").bitcast(FP8X4),
+                scales=ws[:, 0:2, :].rearrange("p c w -> p (c w)"),
+                in_=grs[u][0][:].rearrange("p c w t -> p (c w t)"),
+            )
 
-        tp = psum.tile([P, 5, P], BF16, tag="bank", name="tp")
+        def prep_quant2(u):
+            wc, ws = wcs[u]
+            nc.vector.quantize_mx(
+                out=wc[:, 2, :].bitcast(FP8X4),
+                scales=ws[:, 2, :],
+                in_=grs[u][1][:].rearrange("p w t -> p (w t)"),
+            )
+
+        tp = psum.tile([P, 5, P], BF16, tag="t", name="tp")
         for a in range(4):
             nc.tensor.transpose(tp[:, a, :], x_sb[:, a, :], ident[:])
         nc.tensor.transpose(tp[:, 4, :], blr[:], ident[:])
@@ -116,12 +119,12 @@ def tile_bilinearpairedlayer_kernel(tc, x, W_lin, b_lin, W_bil, b_bil, out):
 
         hpl = const.tile([P, 4, TOK], BF16)
         for j in range(4):
-            hp = psum.tile([P, TOK], F32, tag="bank", name="hp%d" % j)
+            hp = psum.tile([P, TOK], F32, tag="o", name="hp%d" % j)
             nc.tensor.matmul(hp[:], lhsT=wl[:, j * P:(j + 1) * P], rhs=xT[:], start=True, stop=True)
             nc.scalar.activation(out=hpl[:, j, :], in_=hp[:], func=ACT.Relu, bias=blf[:, j:j + 1], scale=1.0)
 
-        grs0 = prep_copies(0)
-        prep_quant(0, grs0, (0, 1))
+        prep_copies(0)
+        prep_quant01(0)
 
         dst, src = regroup_views(hg[1][:], hpl[:])
         nc.vector.tensor_copy(out=dst, in_=src)
@@ -135,67 +138,45 @@ def tile_bilinearpairedlayer_kernel(tc, x, W_lin, b_lin, W_bil, b_bil, out):
                 scales=hs[:, c, :],
                 in_=hg[c][:].rearrange("p w t -> p (w t)"),
             )
-        prep_quant(0, grs0, (2,))
+        prep_quant2(0)
 
-        tcq = const.tile([P, NO * CTX, TOK], U32, align_bytes=64)
-        tsq = const.tile([P, NO * CTX, TOK], U8, align_bytes=64)
+        tcq = const.tile([P, n_units, TOK], U32, align_bytes=64)
+        tsq = const.tile([P, n_units, TOK], U8, align_bytes=64)
         gts = {}
 
-        def stage2(u):
+        def stage2(u, r, engine):
             wc, ws = wcs[u]
-            gt = gtp.tile([P, 4, P, 4], BF16, align_bytes=64, tag="gt", name="gt_%d" % u)
-            gts[u] = gt
-            for r in range(4):
-                bank = psum.tile([P, 4, P], F32, tag="bank", name="t_%d_%d" % (u, r))
-                for tt in range(4):
-                    for c in range(CTX):
-                        nc.tensor.matmul_mx(
-                            out=bank[:, tt, :],
-                            lhsT=wc[:, c, tt * P:(tt + 1) * P].bitcast(FP8X4),
-                            lhsT_scale=ws[:, c, tt * P:(tt + 1) * P],
-                            rhs=hc[:, c, r * P:(r + 1) * P].bitcast(FP8X4),
-                            rhs_scale=hs[:, c, r * P:(r + 1) * P],
-                            start=(c == 0),
-                            stop=(c == CTX - 1),
-                        )
-                if u == len(units) - 1 and r % 2 == 1:
-                    nc.vector.tensor_copy(out=gt[:, r, :, :], in_=bank[:].rearrange("p t r -> p r t"))
-                else:
-                    nc.scalar.copy(out=gt[:, r, :, :], in_=bank[:].rearrange("p t r -> p r t"))
-
-        def quant_t(u):
-            nc.vector.quantize_mx(
-                out=tcq[:, u, :].bitcast(FP8X4),
-                scales=tsq[:, u, :],
-                in_=gts[u][:].rearrange("p r w t -> p (r w t)"),
-            )
-
-        n_units = len(units)
-        for u in range(n_units):
-            if u + 1 < n_units:
-                prep_quant(u + 1, prep_copies(u + 1), (0, 1, 2))
-                o1, g1 = units[u + 1]
-                if g1 == CTX - 1 and o1 + 2 < NO:
-                    for c in range(CTX):
-                        load(o1 + 2, c, 0, H)
-            if u == n_units - 1:
-                quant_t(u - 1)
-                stage2(u)
+            if r == 0:
+                gts[u] = gtp.tile([P, 4, P, 4], BF16, align_bytes=64, tag="gt", name="gt_%d" % u)
+            bank = psum.tile([P, 4, P], F32, tag="t", name="t_%d_%d" % (u, r))
+            for tt in range(4):
+                for c in range(CTX):
+                    nc.tensor.matmul_mx(
+                        out=bank[:, tt, :],
+                        lhsT=wc[:, c, tt * P:(tt + 1) * P].bitcast(FP8X4),
+                        lhsT_scale=ws[:, c, tt * P:(tt + 1) * P],
+                        rhs=hc[:, c, r * P:(r + 1) * P].bitcast(FP8X4),
+                        rhs_scale=hs[:, c, r * P:(r + 1) * P],
+                        start=(c == 0),
+                        stop=(c == CTX - 1),
+                    )
+            if engine == "vector":
+                nc.vector.tensor_copy(out=gts[u][:, r, :, :], in_=bank[:].rearrange("p t r -> p r t"))
             else:
-                stage2(u)
-                if u >= 1:
-                    quant_t(u - 1)
-        bias_t = const.tile([P, P, NO], F32)
-        nc.vector.tensor_copy(out=bias_t[:], in_=bb[:].unsqueeze(1).to_broadcast([P, P, NO]))
-        quant_t(n_units - 1)
+                nc.scalar.copy(out=gts[u][:, r, :, :], in_=bank[:].rearrange("p t r -> p r t"))
+
+        def quant_t(u, r0, r1):
+            nc.vector.quantize_mx(
+                out=tcq[:, u, r0 * P:r1 * P].bitcast(FP8X4),
+                scales=tsq[:, u, r0 * P:r1 * P],
+                in_=gts[u][:, r0:r1, :, :].rearrange("p r w t -> p (r w t)"),
+            )
 
         blocks = [(b, it, jh) for b in range(B) for it in range(2) for jh in range(2)]
         obank = {}
 
         def stage3(k, us):
             b, it, jh = blocks[k]
-            if k not in obank:
-                obank[k] = psum.tile([P, NO, P], F32, tag="bank", name="o_%d" % k)
             ti = b * N + it * P
             tj = b * N + jh * P
             for u in us:
@@ -218,11 +199,39 @@ def tile_bilinearpairedlayer_kernel(tc, x, W_lin, b_lin, W_bil, b_bil, out):
             )
             nc.sync.dma_start(out=out[b, it * P:(it + 1) * P, jh * P:(jh + 1) * P, :], in_=res[:])
 
+        def early3(u):
+            for k in range(4):
+                if u == 0:
+                    obank[k] = psum.tile([P, NO, P], F32, tag="o", name="o_%d" % k)
+                stage3(k, [u])
+
+        last = n_units - 1
+        for u in range(last):
+            prep_copies(u + 1)
+            prep_quant01(u + 1)
+            prep_quant2(u + 1)
+            for r in range(4):
+                stage2(u, r, "scalar")
+            if u >= 1:
+                quant_t(u - 1, 0, 4)
+            if u >= 2:
+                early3(u - 2)
+
+        quant_t(last - 1, 0, 4)
+        bias_t = const.tile([P, P, NO], F32)
+        nc.vector.tensor_copy(out=bias_t[:], in_=bb[:].unsqueeze(1).to_broadcast([P, P, NO]))
+        stage2(last, 0, "scalar")
+        stage2(last, 1, "vector")
+        quant_t(last, 0, 2)
+        early3(last - 2)
+        early3(last - 1)
+        stage2(last, 2, "scalar")
+        stage2(last, 3, "vector")
+        quant_t(last, 2, 4)
+        early3(last)
         for k in range(4):
-            stage3(k, range(n_units - 1))
-        for k in range(4):
-            stage3(k, [n_units - 1])
             finish(k)
         for k in range(4, 8):
+            obank[k] = psum.tile([P, NO, P], F32, tag="t", name="o_%d" % k)
             stage3(k, range(n_units))
             finish(k)

@@ -38,7 +38,7 @@ def tile_bilinearpairedlayer_kernel(tc, x, W_lin, b_lin, W_bil, b_bil, out):
         grpp = ctx.enter_context(tc.tile_pool(name="grpp", bufs=2))
         wcp = ctx.enter_context(tc.tile_pool(name="wcp", bufs=3))
         gtp = ctx.enter_context(tc.tile_pool(name="gtp", bufs=3))
-        resp = ctx.enter_context(tc.tile_pool(name="resp", bufs=4))
+        resp = ctx.enter_context(tc.tile_pool(name="resp", bufs=8))
         psum = ctx.enter_context(tc.psum_pool(name="psum", bufs=4))
 
         units = [(o, g) for o in range(NO) for g in range(CTX)]
@@ -78,13 +78,13 @@ def tile_bilinearpairedlayer_kernel(tc, x, W_lin, b_lin, W_bil, b_bil, out):
         wcs = {}
 
         def prep_copies(u):
-            g2 = grpp.tile([P, NH, 4], BF16, align_bytes=64, tag="grp2", name="grp2_%d" % u)
-            dst, src = regroup_views(g2[:], raw[(u, 2)][:])
-            nc.scalar.copy(out=dst, in_=src)
             g01 = grpp.tile([P, 2, NH, 4], BF16, align_bytes=64, tag="grp01", name="grp01_%d" % u)
             for c in range(2):
                 dst, src = regroup_views(g01[:, c, :, :], raw[(u, c)][:])
                 nc.vector.tensor_copy(out=dst, in_=src)
+            g2 = grpp.tile([P, NH, 4], BF16, align_bytes=64, tag="grp2", name="grp2_%d" % u)
+            dst, src = regroup_views(g2[:], raw[(u, 2)][:])
+            nc.scalar.copy(out=dst, in_=src)
             grs[u] = (g01, g2)
             wc = wcp.tile([P, CTX, NH], U32, align_bytes=64, tag="wc", name="wc_%d" % u)
             ws = wcp.tile([P, CTX, NH], U8, align_bytes=64, tag="ws", name="ws_%d" % u)
@@ -113,9 +113,9 @@ def tile_bilinearpairedlayer_kernel(tc, x, W_lin, b_lin, W_bil, b_bil, out):
             nc.tensor.transpose(tp[:, a, :], x_sb[:, a, :], ident[:])
         nc.tensor.transpose(tp[:, 4, :], blr[:], ident[:])
         xT = const.tile([P, TOK], BF16)
-        nc.vector.tensor_copy(out=xT[:], in_=tp[:, 0:4, :].rearrange("p a t -> p (a t)"))
+        nc.scalar.copy(out=xT[:], in_=tp[:, 0:4, :].rearrange("p a t -> p (a t)"))
         blf = const.tile([P, 4], F32)
-        nc.vector.tensor_copy(out=blf[:], in_=tp[:, 4, 0:4])
+        nc.scalar.copy(out=blf[:], in_=tp[:, 4, 0:4])
 
         hpl = const.tile([P, 4, TOK], BF16)
         for j in range(4):
@@ -123,10 +123,11 @@ def tile_bilinearpairedlayer_kernel(tc, x, W_lin, b_lin, W_bil, b_bil, out):
             nc.tensor.matmul(hp[:], lhsT=wl[:, j * P:(j + 1) * P], rhs=xT[:], start=True, stop=True)
             nc.scalar.activation(out=hpl[:, j, :], in_=hp[:], func=ACT.Relu, bias=blf[:, j:j + 1], scale=1.0)
 
+        dst, src = regroup_views(hg[1][:, N:TOK, :], hpl[:, :, N:TOK])
+        nc.scalar.copy(out=dst, in_=src)
         prep_copies(0)
         prep_quant01(0)
-
-        dst, src = regroup_views(hg[1][:], hpl[:])
+        dst, src = regroup_views(hg[1][:, 0:N, :], hpl[:, :, 0:N])
         nc.vector.tensor_copy(out=dst, in_=src)
         nc.vector.tensor_copy(out=hv[0][:, :, 4:4 * N], in_=hv[1][:, :, 0:4 * N - 4])
         nc.vector.tensor_copy(out=hv[2][:, :, 0:4 * N - 4], in_=hv[1][:, :, 4:4 * N])
@@ -208,30 +209,35 @@ def tile_bilinearpairedlayer_kernel(tc, x, W_lin, b_lin, W_bil, b_bil, out):
         last = n_units - 1
         for u in range(last):
             prep_copies(u + 1)
-            prep_quant01(u + 1)
+            if u >= 1:
+                quant_t(u - 1, 0, 4)
             prep_quant2(u + 1)
+            prep_quant01(u + 1)
             for r in range(4):
                 stage2(u, r, "scalar")
             if u >= 1:
-                quant_t(u - 1, 0, 4)
-            if u >= 2:
-                early3(u - 2)
+                early3(u - 1)
 
         quant_t(last - 1, 0, 4)
         bias_t = const.tile([P, P, NO], F32)
         nc.vector.tensor_copy(out=bias_t[:], in_=bb[:].unsqueeze(1).to_broadcast([P, P, NO]))
-        stage2(last, 0, "scalar")
-        stage2(last, 1, "vector")
+        stage2(last, 0, "vector")
+        stage2(last, 1, "scalar")
         quant_t(last, 0, 2)
-        early3(last - 2)
         early3(last - 1)
         stage2(last, 2, "scalar")
-        stage2(last, 3, "vector")
-        quant_t(last, 2, 4)
+        stage2(last, 3, "scalar")
         early3(last)
-        for k in range(4):
-            finish(k)
+        finish(0)
+        finish(1)
+        quant_t(last, 2, 4)
+        finish(2)
+        finish(3)
         for k in range(4, 8):
             obank[k] = psum.tile([P, NO, P], F32, tag="t", name="o_%d" % k)
-            stage3(k, range(n_units))
-            finish(k)
+            stage3(k, range(last))
+            if k > 4:
+                stage3(k - 1, [last])
+                finish(k - 1)
+        stage3(7, [last])
+        finish(7)

@@ -37,7 +37,7 @@ def tile_bilinearpairedlayer_kernel(tc, x, W_lin, b_lin, W_bil, b_bil, out):
         rawp = ctx.enter_context(tc.tile_pool(name="rawp", bufs=CTX * RAW_UNITS))
         grpp = ctx.enter_context(tc.tile_pool(name="grpp", bufs=2))
         wcp = ctx.enter_context(tc.tile_pool(name="wcp", bufs=3))
-        gtp = ctx.enter_context(tc.tile_pool(name="gtp", bufs=3))
+        gtp = ctx.enter_context(tc.tile_pool(name="gtp", bufs=4))
         resp = ctx.enter_context(tc.tile_pool(name="resp", bufs=8))
         psum = ctx.enter_context(tc.psum_pool(name="psum", bufs=4))
 
@@ -50,9 +50,7 @@ def tile_bilinearpairedlayer_kernel(tc, x, W_lin, b_lin, W_bil, b_bil, out):
         nc.sync.dma_start(out=wl[:], in_=W_lin)
         blr = const.tile([P, P], BF16)
         nc.vector.memset(blr[:], 0.0)
-        nc.sync.dma_start(out=blr[0:4, :], in_=b_lin.rearrange("(j p) -> j p", p=P))
-        bb = const.tile([P, NO], BF16)
-        nc.scalar.dma_start(out=bb[:], in_=b_bil.partition_broadcast(P))
+        nc.scalar.dma_start(out=blr[0:4, :], in_=b_lin.rearrange("(j p) -> j p", p=P))
 
         raw = {}
 
@@ -209,29 +207,33 @@ def tile_bilinearpairedlayer_kernel(tc, x, W_lin, b_lin, W_bil, b_bil, out):
         last = n_units - 1
         for u in range(last):
             prep_copies(u + 1)
-            if u >= 1:
+            if 1 <= u < last - 1:
                 quant_t(u - 1, 0, 4)
             prep_quant2(u + 1)
             prep_quant01(u + 1)
             for r in range(4):
                 stage2(u, r, "scalar")
-            if u >= 1:
+            if 1 <= u < last - 1:
                 early3(u - 1)
 
+        bb = const.tile([P, NO], BF16)
+        nc.sync.dma_start(out=bb[:], in_=b_bil.partition_broadcast(P))
+        quant_t(last - 2, 0, 4)
         quant_t(last - 1, 0, 4)
         bias_t = const.tile([P, P, NO], F32)
         nc.vector.tensor_copy(out=bias_t[:], in_=bb[:].unsqueeze(1).to_broadcast([P, P, NO]))
         stage2(last, 0, "vector")
         stage2(last, 1, "scalar")
         quant_t(last, 0, 2)
+        early3(last - 2)
         early3(last - 1)
         stage2(last, 2, "scalar")
-        stage2(last, 3, "scalar")
         early3(last)
+        stage2(last, 3, "scalar")
         finish(0)
         finish(1)
-        quant_t(last, 2, 4)
         finish(2)
+        quant_t(last, 2, 4)
         finish(3)
         for k in range(4, 8):
             obank[k] = psum.tile([P, NO, P], F32, tag="t", name="o_%d" % k)

@@ -37,7 +37,7 @@ def tile_bilinearpairedlayer_kernel(tc, x, W_lin, b_lin, W_bil, b_bil, out):
         rawp = ctx.enter_context(tc.tile_pool(name="rawp", bufs=CTX * RAW_UNITS))
         grpp = ctx.enter_context(tc.tile_pool(name="grpp", bufs=2))
         wcp = ctx.enter_context(tc.tile_pool(name="wcp", bufs=3))
-        gtp = ctx.enter_context(tc.tile_pool(name="gtp", bufs=4))
+        gtp = ctx.enter_context(tc.tile_pool(name="gtp", bufs=3))
         resp = ctx.enter_context(tc.tile_pool(name="resp", bufs=8))
         psum = ctx.enter_context(tc.psum_pool(name="psum", bufs=4))
 
@@ -50,7 +50,7 @@ def tile_bilinearpairedlayer_kernel(tc, x, W_lin, b_lin, W_bil, b_bil, out):
         nc.sync.dma_start(out=wl[:], in_=W_lin)
         blr = const.tile([P, P], BF16)
         nc.vector.memset(blr[:], 0.0)
-        nc.scalar.dma_start(out=blr[0:4, :], in_=b_lin.rearrange("(j p) -> j p", p=P))
+        nc.sync.dma_start(out=blr[0:4, :], in_=b_lin.rearrange("(j p) -> j p", p=P))
 
         raw = {}
 
@@ -207,33 +207,31 @@ def tile_bilinearpairedlayer_kernel(tc, x, W_lin, b_lin, W_bil, b_bil, out):
         last = n_units - 1
         for u in range(last):
             prep_copies(u + 1)
-            if 1 <= u < last - 1:
+            if u >= 1:
                 quant_t(u - 1, 0, 4)
             prep_quant2(u + 1)
             prep_quant01(u + 1)
             for r in range(4):
                 stage2(u, r, "scalar")
-            if 1 <= u < last - 1:
+            if u >= 1:
                 early3(u - 1)
 
         bb = const.tile([P, NO], BF16)
         nc.sync.dma_start(out=bb[:], in_=b_bil.partition_broadcast(P))
-        quant_t(last - 2, 0, 4)
         quant_t(last - 1, 0, 4)
         bias_t = const.tile([P, P, NO], F32)
         nc.vector.tensor_copy(out=bias_t[:], in_=bb[:].unsqueeze(1).to_broadcast([P, P, NO]))
         stage2(last, 0, "vector")
         stage2(last, 1, "scalar")
         quant_t(last, 0, 2)
-        early3(last - 2)
         early3(last - 1)
         stage2(last, 2, "scalar")
-        early3(last)
         stage2(last, 3, "scalar")
+        early3(last)
         finish(0)
         finish(1)
-        finish(2)
         quant_t(last, 2, 4)
+        finish(2)
         finish(3)
         for k in range(4, 8):
             obank[k] = psum.tile([P, NO, P], F32, tag="t", name="o_%d" % k)

@@ -209,8 +209,8 @@ def tile_bilinearpairedlayer_kernel(tc, x, W_lin, b_lin, W_bil, b_bil, out):
             prep_copies(u + 1)
             if u >= 1:
                 quant_t(u - 1, 0, 4)
-            prep_quant2(u + 1)
             prep_quant01(u + 1)
+            prep_quant2(u + 1)
             for r in range(4):
                 stage2(u, r, "scalar")
             if u >= 1:

@@ -38,14 +38,14 @@ def tile_bilinearpairedlayer_kernel(tc, x, W_lin, b_lin, W_bil, b_bil, out):
         grpp = ctx.enter_context(tc.tile_pool(name="grpp", bufs=2))
         wcp = ctx.enter_context(tc.tile_pool(name="wcp", bufs=3))
         gtp = ctx.enter_context(tc.tile_pool(name="gtp", bufs=3))
-        resp = ctx.enter_context(tc.tile_pool(name="resp", bufs=8))
+        resp = ctx.enter_context(tc.tile_pool(name="resp", bufs=4))
         psum = ctx.enter_context(tc.psum_pool(name="psum", bufs=4))
 
         units = [(o, g) for o in range(NO) for g in range(CTX)]
         n_units = len(units)
 
-        x_sb = const.tile([P, 4, NI], BF16)
-        nc.sync.dma_start(out=x_sb[:], in_=x.flatten_outer_dims().rearrange("(a p) n -> p a n", p=P))
+        x_sb = const.tile([P, B, 2 * NI], BF16)
+        nc.sync.dma_start(out=x_sb[:], in_=x.rearrange("b (q r) n -> q b (r n)", r=2))
         wl = const.tile([P, NH], BF16)
         nc.sync.dma_start(out=wl[:], in_=W_lin)
         blr = const.tile([P, P], BF16)
@@ -67,10 +67,9 @@ def tile_bilinearpairedlayer_kernel(tc, x, W_lin, b_lin, W_bil, b_bil, out):
         ident = const.tile([P, P], BF16)
         make_identity(nc, ident[:])
 
-        hg = [const.tile([P, TOK, 4], BF16, align_bytes=64, name="hg%d" % c) for c in range(CTX)]
-        hv = [hg[c][:].rearrange("p (b i) t -> p b (i t)", b=B) for c in range(CTX)]
-        nc.vector.memset(hv[0][:, :, 0:4], 0.0)
-        nc.vector.memset(hv[2][:, :, 4 * N - 4:4 * N], 0.0)
+        hg = const.tile([P, B, 4, 4 * P], BF16, align_bytes=64)
+        nc.vector.memset(hg[:, :, 0, 0:4], 0.0)
+        nc.vector.memset(hg[:, :, 3, 4 * P - 4:4 * P], 0.0)
 
         grs = {}
         wcs = {}
@@ -108,7 +107,7 @@ def tile_bilinearpairedlayer_kernel(tc, x, W_lin, b_lin, W_bil, b_bil, out):
 
         tp = psum.tile([P, 5, P], BF16, tag="t", name="tp")
         for a in range(4):
-            nc.tensor.transpose(tp[:, a, :], x_sb[:, a, :], ident[:])
+            nc.tensor.transpose(tp[:, a, :], x_sb[:, a // 2, (a % 2) * NI:(a % 2 + 1) * NI], ident[:])
         nc.tensor.transpose(tp[:, 4, :], blr[:], ident[:])
         xT = const.tile([P, TOK], BF16)
         nc.scalar.copy(out=xT[:], in_=tp[:, 0:4, :].rearrange("p a t -> p (a t)"))
@@ -121,21 +120,24 @@ def tile_bilinearpairedlayer_kernel(tc, x, W_lin, b_lin, W_bil, b_bil, out):
             nc.tensor.matmul(hp[:], lhsT=wl[:, j * P:(j + 1) * P], rhs=xT[:], start=True, stop=True)
             nc.scalar.activation(out=hpl[:, j, :], in_=hp[:], func=ACT.Relu, bias=blf[:, j:j + 1], scale=1.0)
 
-        dst, src = regroup_views(hg[1][:, N:TOK, :], hpl[:, :, N:TOK])
+        def h_regroup(b):
+            return regroup_views(hg[:, b, 1:3, :].rearrange("p e (q t) -> p (e q) t", t=4), hpl[:, :, b * N:(b + 1) * N])
+
+        dst, src = h_regroup(1)
         nc.scalar.copy(out=dst, in_=src)
         prep_copies(0)
         prep_quant01(0)
-        dst, src = regroup_views(hg[1][:, 0:N, :], hpl[:, :, 0:N])
+        dst, src = h_regroup(0)
         nc.vector.tensor_copy(out=dst, in_=src)
-        nc.vector.tensor_copy(out=hv[0][:, :, 4:4 * N], in_=hv[1][:, :, 0:4 * N - 4])
-        nc.vector.tensor_copy(out=hv[2][:, :, 0:4 * N - 4], in_=hv[1][:, :, 4:4 * N])
-        hc = const.tile([P, CTX, TOK], U32, align_bytes=64)
-        hs = const.tile([P, CTX, TOK], U8, align_bytes=64)
-        for c in (1, 0, 2):
+        nc.vector.tensor_copy(out=hg[:, :, 0, 4:4 * P], in_=hg[:, :, 2, 0:4 * P - 4])
+        nc.vector.tensor_copy(out=hg[:, :, 3, 0:4 * P - 4], in_=hg[:, :, 1, 4:4 * P])
+        hc = const.tile([P, B, 4, P], U32, align_bytes=64)
+        hs = const.tile([P, B, 4, P], U8, align_bytes=64)
+        for b in range(B):
             nc.vector.quantize_mx(
-                out=hc[:, c, :].bitcast(FP8X4),
-                scales=hs[:, c, :],
-                in_=hg[c][:].rearrange("p w t -> p (w t)"),
+                out=hc[:, b, :, :].rearrange("p e q -> p (e q)").bitcast(FP8X4),
+                scales=hs[:, b, :, :].rearrange("p e q -> p (e q)"),
+                in_=hg[:, b, :, :].rearrange("p e x -> p (e x)"),
             )
         prep_quant2(0)
 
@@ -154,8 +156,8 @@ def tile_bilinearpairedlayer_kernel(tc, x, W_lin, b_lin, W_bil, b_bil, out):
                         out=bank[:, tt, :],
                         lhsT=wc[:, c, tt * P:(tt + 1) * P].bitcast(FP8X4),
                         lhsT_scale=ws[:, c, tt * P:(tt + 1) * P],
-                        rhs=hc[:, c, r * P:(r + 1) * P].bitcast(FP8X4),
-                        rhs_scale=hs[:, c, r * P:(r + 1) * P],
+                        rhs=hc[:, r // 2, r % 2 + c, :].bitcast(FP8X4),
+                        rhs_scale=hs[:, r // 2, r % 2 + c, :],
                         start=(c == 0),
                         stop=(c == CTX - 1),
                     )
@@ -171,32 +173,39 @@ def tile_bilinearpairedlayer_kernel(tc, x, W_lin, b_lin, W_bil, b_bil, out):
                 in_=gts[u][:, r0:r1, :, :].rearrange("p r w t -> p (r w t)"),
             )
 
-        blocks = [(b, it, jh) for b in range(B) for it in range(2) for jh in range(2)]
+        blocks = [(b, ri, rj) for b in range(B) for ri in range(2) for rj in range(2)]
         obank = {}
+        results = {}
 
         def stage3(k, us):
-            b, it, jh = blocks[k]
-            ti = b * N + it * P
-            tj = b * N + jh * P
+            b, ri, rj = blocks[k]
+            ti = (b * 2 + ri) * P
             for u in us:
                 o, g = units[u]
                 nc.tensor.matmul_mx(
                     out=obank[k][:, o, :],
                     lhsT=tcq[:, u, ti:ti + P].bitcast(FP8X4),
                     lhsT_scale=tsq[:, u, ti:ti + P],
-                    rhs=hc[:, g, tj:tj + P].bitcast(FP8X4),
-                    rhs_scale=hs[:, g, tj:tj + P],
+                    rhs=hc[:, b, rj + g, :].bitcast(FP8X4),
+                    rhs_scale=hs[:, b, rj + g, :],
                     start=(g == 0),
                     stop=(g == CTX - 1),
                 )
 
         def finish(k):
-            b, it, jh = blocks[k]
-            res = resp.tile([P, P, NO], F32, tag="res", name="res_%d" % k)
+            b, ri, rj = blocks[k]
+            if rj == 0:
+                results[(b, ri)] = resp.tile([P, P, 2, NO], F32, tag="res", name="res_%d" % k)
+            res = results[(b, ri)]
             nc.vector.tensor_tensor(
-                out=res[:], in0=obank[k][:].rearrange("p o j -> p j o"), in1=bias_t[:], op=ALU.add
+                out=res[:, :, rj, :],
+                in0=obank[k][:].rearrange("p o j -> p j o"),
+                in1=bb[:].unsqueeze(1).to_broadcast([P, P, NO]),
+                op=ALU.add,
             )
-            nc.sync.dma_start(out=out[b, it * P:(it + 1) * P, jh * P:(jh + 1) * P, :], in_=res[:])
+            if rj == 1:
+                dst = out[b].rearrange("(q r) j o -> r q (j o)", r=2)[ri]
+                nc.sync.dma_start(out=dst, in_=res[:].rearrange("p q r o -> p (q r o)"))
 
         def early3(u):
             for k in range(4):
@@ -219,8 +228,6 @@ def tile_bilinearpairedlayer_kernel(tc, x, W_lin, b_lin, W_bil, b_bil, out):
         bb = const.tile([P, NO], BF16)
         nc.sync.dma_start(out=bb[:], in_=b_bil.partition_broadcast(P))
         quant_t(last - 1, 0, 4)
-        bias_t = const.tile([P, P, NO], F32)
-        nc.vector.tensor_copy(out=bias_t[:], in_=bb[:].unsqueeze(1).to_broadcast([P, P, NO]))
         stage2(last, 0, "vector")
         stage2(last, 1, "scalar")
         quant_t(last, 0, 2)

@@ -17,8 +17,15 @@ CTX = 3
 H = NH * CTX
 TOK = B * N
 FLOPS = 2 * TOK * NI * NH + 2 * TOK * H * NO * H + 2 * B * N * NO * N * H
-PIN = True
 RAW_UNITS = 7
+
+
+def v_cols(u):
+    return NH if u in (0, 11) else 448
+
+
+WHOLE = [(0, NH)]
+LAST = [(0, 256), (256, 384), (384, 512)]
 
 
 def regroup_views(dst, src):
@@ -31,8 +38,7 @@ def regroup_views(dst, src):
 def tile_bilinearpairedlayer_kernel(tc, x, W_lin, b_lin, W_bil, b_bil, out):
     nc = tc.nc
     with ExitStack() as ctx:
-        if PIN:
-            ctx.enter_context(tc.manual_schedule())
+        ctx.enter_context(tc.manual_schedule())
         const = ctx.enter_context(tc.tile_pool(name="const", bufs=1))
         rawp = ctx.enter_context(tc.tile_pool(name="rawp", bufs=CTX * RAW_UNITS))
         grpp = ctx.enter_context(tc.tile_pool(name="grpp", bufs=2))
@@ -43,6 +49,7 @@ def tile_bilinearpairedlayer_kernel(tc, x, W_lin, b_lin, W_bil, b_bil, out):
 
         units = [(o, g) for o in range(NO) for g in range(CTX)]
         n_units = len(units)
+        last = n_units - 1
 
         x_sb = const.tile([P, B, 2 * NI], BF16)
         nc.sync.dma_start(out=x_sb[:], in_=x.rearrange("b (q r) n -> q b (r n)", r=2))
@@ -74,36 +81,53 @@ def tile_bilinearpairedlayer_kernel(tc, x, W_lin, b_lin, W_bil, b_bil, out):
         grs = {}
         wcs = {}
 
-        def prep_copies(u):
-            g01 = grpp.tile([P, 2, NH, 4], BF16, align_bytes=64, tag="grp01", name="grp01_%d" % u)
-            for c in range(2):
-                dst, src = regroup_views(g01[:, c, :, :], raw[(u, c)][:])
-                nc.vector.tensor_copy(out=dst, in_=src)
-            g2 = grpp.tile([P, NH, 4], BF16, align_bytes=64, tag="grp2", name="grp2_%d" % u)
-            dst, src = regroup_views(g2[:], raw[(u, 2)][:])
-            nc.scalar.copy(out=dst, in_=src)
+        def chunks_of(u):
+            return LAST if u == last else WHOLE
+
+        def alloc(u):
+            g01 = grpp.tile([P, 2 * NH * 4], BF16, align_bytes=64, tag="grp01", name="grp01_%d" % u)
+            g2 = grpp.tile([P, NH * 4], BF16, align_bytes=64, tag="grp2", name="grp2_%d" % u)
             grs[u] = (g01, g2)
-            wc = wcp.tile([P, CTX, NH], U32, align_bytes=64, tag="wc", name="wc_%d" % u)
-            ws = wcp.tile([P, CTX, NH], U8, align_bytes=64, tag="ws", name="ws_%d" % u)
+            wc = wcp.tile([P, CTX * NH], U32, align_bytes=64, tag="wc", name="wc_%d" % u)
+            ws = wcp.tile([P, CTX * NH], U8, align_bytes=64, tag="ws", name="ws_%d" % u)
             wcs[u] = (wc, ws)
-            if u + RAW_UNITS < n_units:
-                load(u + RAW_UNITS)
 
-        def prep_quant01(u):
-            wc, ws = wcs[u]
-            nc.vector.quantize_mx(
-                out=wc[:, 0:2, :].rearrange("p c w -> p (c w)").bitcast(FP8X4),
-                scales=ws[:, 0:2, :].rearrange("p c w -> p (c w)"),
-                in_=grs[u][0][:].rearrange("p c w t -> p (c w t)"),
-            )
+        def grouped(u, c, g0, g1):
+            if c == 2:
+                return grs[u][1][:, 4 * g0:4 * g1].rearrange("p (w t) -> p w t", t=4)
+            base = 8 * g0 + c * 4 * (g1 - g0)
+            return grs[u][0][:, base:base + 4 * (g1 - g0)].rearrange("p (w t) -> p w t", t=4)
 
-        def prep_quant2(u):
+        def copies_v(u, g0, g1):
+            split = min(g1, max(g0, v_cols(u)))
+            for c, e in ((0, g1), (1, split)):
+                if e > g0:
+                    dst, src = regroup_views(grouped(u, c, g0, g1)[:, 0:e - g0, :], raw[(u, c)][:, :, g0:e])
+                    nc.vector.tensor_copy(out=dst, in_=src)
+
+        def copies_s(u, g0, g1):
+            split = min(g1, max(g0, v_cols(u)))
+            for c, s in ((1, split), (2, g0)):
+                if s < g1:
+                    dst, src = regroup_views(grouped(u, c, g0, g1)[:, s - g0:g1 - g0, :], raw[(u, c)][:, :, s:g1])
+                    nc.scalar.copy(out=dst, in_=src)
+
+        def quant_w(u, g0, g1, cs):
             wc, ws = wcs[u]
-            nc.vector.quantize_mx(
-                out=wc[:, 2, :].bitcast(FP8X4),
-                scales=ws[:, 2, :],
-                in_=grs[u][1][:].rearrange("p w t -> p (w t)"),
-            )
+            w = g1 - g0
+            a = CTX * g0 + cs[0] * w
+            e = a + len(cs) * w
+            if cs[0] == 2:
+                src = grs[u][1][:, 4 * g0:4 * g1]
+            else:
+                src = grs[u][0][:, 8 * g0:8 * g1]
+            nc.vector.quantize_mx(out=wc[:, a:e].bitcast(FP8X4), scales=ws[:, a:e], in_=src)
+
+        def w_cols(u, c, tt):
+            for g0, g1 in chunks_of(u):
+                if g0 <= tt * P < g1:
+                    a = CTX * g0 + c * (g1 - g0) + tt * P - g0
+                    return slice(a, a + P)
 
         tp = psum.tile([P, 5, P], BF16, tag="t", name="tp")
         for a in range(4):
@@ -125,8 +149,11 @@ def tile_bilinearpairedlayer_kernel(tc, x, W_lin, b_lin, W_bil, b_bil, out):
 
         dst, src = h_regroup(1)
         nc.scalar.copy(out=dst, in_=src)
-        prep_copies(0)
-        prep_quant01(0)
+        alloc(0)
+        copies_v(0, 0, NH)
+        copies_s(0, 0, NH)
+        load(RAW_UNITS)
+        quant_w(0, 0, NH, (0, 1))
         dst, src = h_regroup(0)
         nc.vector.tensor_copy(out=dst, in_=src)
         nc.vector.tensor_copy(out=hg[:, :, 0, 4:4 * P], in_=hg[:, :, 2, 0:4 * P - 4])
@@ -139,32 +166,38 @@ def tile_bilinearpairedlayer_kernel(tc, x, W_lin, b_lin, W_bil, b_bil, out):
                 scales=hs[:, b, :, :].rearrange("p e q -> p (e q)"),
                 in_=hg[:, b, :, :].rearrange("p e x -> p (e x)"),
             )
-        prep_quant2(0)
+        quant_w(0, 0, NH, (2,))
 
         tcq = const.tile([P, n_units, TOK], U32, align_bytes=64)
         tsq = const.tile([P, n_units, TOK], U8, align_bytes=64)
         gts = {}
+        banks = {}
 
-        def stage2(u, r, engine):
+        def stage2(u, r, tts):
             wc, ws = wcs[u]
-            if r == 0:
+            if u not in gts:
                 gts[u] = gtp.tile([P, 4, P, 4], BF16, align_bytes=64, tag="gt", name="gt_%d" % u)
-            bank = psum.tile([P, 4, P], F32, tag="t", name="t_%d_%d" % (u, r))
-            for tt in range(4):
+            if (u, r) not in banks:
+                banks[(u, r)] = psum.tile([P, 4, P], F32, tag="t", name="t_%d_%d" % (u, r))
+            for tt in tts:
                 for c in range(CTX):
+                    cols = w_cols(u, c, tt)
                     nc.tensor.matmul_mx(
-                        out=bank[:, tt, :],
-                        lhsT=wc[:, c, tt * P:(tt + 1) * P].bitcast(FP8X4),
-                        lhsT_scale=ws[:, c, tt * P:(tt + 1) * P],
+                        out=banks[(u, r)][:, tt, :],
+                        lhsT=wc[:, cols].bitcast(FP8X4),
+                        lhsT_scale=ws[:, cols],
                         rhs=hc[:, r // 2, r % 2 + c, :].bitcast(FP8X4),
                         rhs_scale=hs[:, r // 2, r % 2 + c, :],
                         start=(c == 0),
                         stop=(c == CTX - 1),
                     )
+
+        def copy_t(u, r, engine):
+            src = banks[(u, r)][:].rearrange("p t r -> p r t")
             if engine == "vector":
-                nc.vector.tensor_copy(out=gts[u][:, r, :, :], in_=bank[:].rearrange("p t r -> p r t"))
+                nc.vector.tensor_copy(out=gts[u][:, r, :, :], in_=src)
             else:
-                nc.scalar.copy(out=gts[u][:, r, :, :], in_=bank[:].rearrange("p t r -> p r t"))
+                nc.scalar.copy(out=gts[u][:, r, :, :], in_=src)
 
         def quant_t(u, r0, r1):
             nc.vector.quantize_mx(
@@ -177,9 +210,11 @@ def tile_bilinearpairedlayer_kernel(tc, x, W_lin, b_lin, W_bil, b_bil, out):
         obank = {}
         results = {}
 
-        def stage3(k, us):
+        def stage3(k, us, tag):
             b, ri, rj = blocks[k]
             ti = (b * 2 + ri) * P
+            if k not in obank:
+                obank[k] = psum.tile([P, NO, P], F32, tag=tag, name="o_%d" % k)
             for u in us:
                 o, g = units[u]
                 nc.tensor.matmul_mx(
@@ -192,59 +227,81 @@ def tile_bilinearpairedlayer_kernel(tc, x, W_lin, b_lin, W_bil, b_bil, out):
                     stop=(g == CTX - 1),
                 )
 
-        def finish(k):
+        def finish(k, cuts):
             b, ri, rj = blocks[k]
             if rj == 0:
                 results[(b, ri)] = resp.tile([P, P, 2, NO], F32, tag="res", name="res_%d" % k)
             res = results[(b, ri)]
-            nc.vector.tensor_tensor(
-                out=res[:, :, rj, :],
-                in0=obank[k][:].rearrange("p o j -> p j o"),
-                in1=bb[:].unsqueeze(1).to_broadcast([P, P, NO]),
-                op=ALU.add,
-            )
-            if rj == 1:
-                dst = out[b].rearrange("(q r) j o -> r q (j o)", r=2)[ri]
-                nc.sync.dma_start(out=dst, in_=res[:].rearrange("p q r o -> p (q r o)"))
+            for q0, q1 in zip(cuts, cuts[1:]):
+                nc.vector.tensor_tensor(
+                    out=res[:, q0:q1, rj, :],
+                    in0=obank[k][:, :, q0:q1].rearrange("p o j -> p j o"),
+                    in1=bb[:].unsqueeze(1).to_broadcast([P, q1 - q0, NO]),
+                    op=ALU.add,
+                )
+                if rj == 1:
+                    dst = out[b].rearrange("(q r) j o -> r q (j o)", r=2)[ri]
+                    nc.sync.dma_start(
+                        out=dst[:, q0 * 2 * NO:q1 * 2 * NO],
+                        in_=res[:, q0:q1, :, :].rearrange("p q r o -> p (q r o)"),
+                    )
 
         def early3(u):
             for k in range(4):
-                if u == 0:
-                    obank[k] = psum.tile([P, NO, P], F32, tag="o", name="o_%d" % k)
-                stage3(k, [u])
+                stage3(k, [u], "o")
 
-        last = n_units - 1
-        for u in range(last):
-            prep_copies(u + 1)
+        for u in range(last - 1):
+            alloc(u + 1)
+            copies_v(u + 1, 0, NH)
+            copies_s(u + 1, 0, NH)
+            if u + 1 + RAW_UNITS < n_units:
+                load(u + 1 + RAW_UNITS)
             if u >= 1:
                 quant_t(u - 1, 0, 4)
-            prep_quant01(u + 1)
-            prep_quant2(u + 1)
+            quant_w(u + 1, 0, NH, (0, 1))
+            quant_w(u + 1, 0, NH, (2,))
             for r in range(4):
-                stage2(u, r, "scalar")
+                stage2(u, r, range(4))
+                copy_t(u, r, "scalar")
             if u >= 1:
                 early3(u - 1)
 
         bb = const.tile([P, NO], BF16)
         nc.sync.dma_start(out=bb[:], in_=b_bil.partition_broadcast(P))
-        quant_t(last - 1, 0, 4)
-        stage2(last, 0, "vector")
-        stage2(last, 1, "scalar")
+
+        u = last - 1
+        alloc(last)
+        for i, (g0, g1) in enumerate(LAST):
+            copies_v(last, g0, g1)
+            copies_s(last, g0, g1)
+            if i == 0:
+                quant_t(u - 1, 0, 4)
+            if i >= 1:
+                quant_w(last, LAST[i - 1][0], LAST[i - 1][1], (0, 1))
+                quant_w(last, LAST[i - 1][0], LAST[i - 1][1], (2,))
+            if i < 2:
+                for r in (2 * i, 2 * i + 1):
+                    stage2(u, r, range(4))
+                    copy_t(u, r, "scalar")
+        quant_w(last, LAST[-1][0], LAST[-1][1], (0, 1))
+        quant_w(last, LAST[-1][0], LAST[-1][1], (2,))
+        early3(u - 1)
+        quant_t(u, 0, 4)
+        for g0, g1 in LAST:
+            for r in range(4):
+                stage2(last, r, range(g0 // P, g1 // P))
+        for r in range(4):
+            copy_t(last, r, ("vector", "scalar")[r % 2])
         quant_t(last, 0, 2)
-        early3(last - 1)
-        stage2(last, 2, "scalar")
-        stage2(last, 3, "scalar")
-        early3(last)
-        finish(0)
-        finish(1)
         quant_t(last, 2, 4)
-        finish(2)
-        finish(3)
-        for k in range(4, 8):
-            obank[k] = psum.tile([P, NO, P], F32, tag="t", name="o_%d" % k)
-            stage3(k, range(last))
-            if k > 4:
-                stage3(k - 1, [last])
-                finish(k - 1)
-        stage3(7, [last])
-        finish(7)
+        early3(u)
+        stage3(4, range(last), "t")
+        early3(last)
+        for k in range(4):
+            finish(k, (0, P))
+        for k in range(5, 8):
+            stage3(k - 1, [last], "t")
+            stage3(k, range(last), "t")
+            finish(k - 1, (0, P))
+        stage3(7, [last], "t")
+        finish(7, (0, P // 2, P))

from contextlib import ExitStack

import concourse.mybir as mybir
from concourse.masks import make_identity

BF16 = mybir.dt.bfloat16
F32 = mybir.dt.float32
U32 = mybir.dt.uint32
U8 = mybir.dt.uint8
FP8X4 = mybir.dt.float8_e4m3fn_x4
ACT = mybir.ActivationFunctionType
ALU = mybir.AluOpType

P = 128
B, N, NI, NH, NO = 2, 256, 128, 512, 4
CTX = 3
H = NH * CTX
TOK = B * N
FLOPS = 2 * TOK * NI * NH + 2 * TOK * H * NO * H + 2 * B * N * NO * N * H
RAW_UNITS = 7


def v_cols(u):
    return NH if u in (0, 11) else 448


WHOLE = [(0, NH)]
LAST = [(0, 256), (256, 384), (384, 512)]


def regroup_views(dst, src):
    return (
        dst.rearrange("p (c i) t -> p c t i", i=4),
        src.rearrange("p t (c i) -> p c t i", i=4),
    )


def tile_bilinearpairedlayer_kernel(tc, x, W_lin, b_lin, W_bil, b_bil, out):
    nc = tc.nc
    with ExitStack() as ctx:
        ctx.enter_context(tc.manual_schedule())
        const = ctx.enter_context(tc.tile_pool(name="const", bufs=1))
        rawp = ctx.enter_context(tc.tile_pool(name="rawp", bufs=CTX * RAW_UNITS))
        grpp = ctx.enter_context(tc.tile_pool(name="grpp", bufs=2))
        wcp = ctx.enter_context(tc.tile_pool(name="wcp", bufs=3))
        gtp = ctx.enter_context(tc.tile_pool(name="gtp", bufs=3))
        resp = ctx.enter_context(tc.tile_pool(name="resp", bufs=4))
        psum = ctx.enter_context(tc.psum_pool(name="psum", bufs=4))

        units = [(o, g) for o in range(NO) for g in range(CTX)]
        n_units = len(units)
        last = n_units - 1

        x_sb = const.tile([P, B, 2 * NI], BF16)
        nc.sync.dma_start(out=x_sb[:], in_=x.rearrange("b (q r) n -> q b (r n)", r=2))
        wl = const.tile([P, NH], BF16)
        nc.sync.dma_start(out=wl[:], in_=W_lin)
        blr = const.tile([P, P], BF16)
        nc.vector.memset(blr[:], 0.0)
        nc.sync.dma_start(out=blr[0:4, :], in_=b_lin.rearrange("(j p) -> j p", p=P))

        raw = {}

        def load(u):
            o, g = units[u]
            for c in range(CTX):
                raw[(u, c)] = rawp.tile([P, 4, NH], BF16, tag="raw", name="raw_%d_%d" % (u, c))
                src = W_bil[o, c * NH:(c + 1) * NH, g * NH:(g + 1) * NH]
                nc.sync.dma_start(out=raw[(u, c)][:], in_=src.rearrange("(j p) g -> p j g", p=P))

        for u in range(RAW_UNITS):
            load(u)

        ident = const.tile([P, P], BF16)
        make_identity(nc, ident[:])

        hg = const.tile([P, B, 4, 4 * P], BF16, align_bytes=64)
        nc.vector.memset(hg[:, :, 0, 0:4], 0.0)
        nc.vector.memset(hg[:, :, 3, 4 * P - 4:4 * P], 0.0)

        grs = {}
        wcs = {}

        def chunks_of(u):
            return LAST if u == last else WHOLE

        def alloc(u):
            g01 = grpp.tile([P, 2 * NH * 4], BF16, align_bytes=64, tag="grp01", name="grp01_%d" % u)
            g2 = grpp.tile([P, NH * 4], BF16, align_bytes=64, tag="grp2", name="grp2_%d" % u)
            grs[u] = (g01, g2)
            wc = wcp.tile([P, CTX * NH], U32, align_bytes=64, tag="wc", name="wc_%d" % u)
            ws = wcp.tile([P, CTX * NH], U8, align_bytes=64, tag="ws", name="ws_%d" % u)
            wcs[u] = (wc, ws)

        def grouped(u, c, g0, g1):
            if c == 2:
                return grs[u][1][:, 4 * g0:4 * g1].rearrange("p (w t) -> p w t", t=4)
            base = 8 * g0 + c * 4 * (g1 - g0)
            return grs[u][0][:, base:base + 4 * (g1 - g0)].rearrange("p (w t) -> p w t", t=4)

        def copies_v(u, g0, g1):
            split = min(g1, max(g0, v_cols(u)))
            for c, e in ((0, g1), (1, split)):
                if e > g0:
                    dst, src = regroup_views(grouped(u, c, g0, g1)[:, 0:e - g0, :], raw[(u, c)][:, :, g0:e])
                    nc.vector.tensor_copy(out=dst, in_=src)

        def copies_s(u, g0, g1):
            split = min(g1, max(g0, v_cols(u)))
            for c, s in ((1, split), (2, g0)):
                if s < g1:
                    dst, src = regroup_views(grouped(u, c, g0, g1)[:, s - g0:g1 - g0, :], raw[(u, c)][:, :, s:g1])
                    nc.scalar.copy(out=dst, in_=src)

        def quant_w(u, g0, g1, cs):
            wc, ws = wcs[u]
            w = g1 - g0
            a = CTX * g0 + cs[0] * w
            e = a + len(cs) * w
            if cs[0] == 2:
                src = grs[u][1][:, 4 * g0:4 * g1]
            else:
                src = grs[u][0][:, 8 * g0:8 * g1]
            nc.vector.quantize_mx(out=wc[:, a:e].bitcast(FP8X4), scales=ws[:, a:e], in_=src)

        def w_cols(u, c, tt):
            for g0, g1 in chunks_of(u):
                if g0 <= tt * P < g1:
                    a = CTX * g0 + c * (g1 - g0) + tt * P - g0
                    return slice(a, a + P)

        tp = psum.tile([P, 5, P], BF16, tag="t", name="tp")
        for a in range(4):
            nc.tensor.transpose(tp[:, a, :], x_sb[:, a // 2, (a % 2) * NI:(a % 2 + 1) * NI], ident[:])
        nc.tensor.transpose(tp[:, 4, :], blr[:], ident[:])
        xT = const.tile([P, TOK], BF16)
        nc.scalar.copy(out=xT[:], in_=tp[:, 0:4, :].rearrange("p a t -> p (a t)"))
        blf = const.tile([P, 4], F32)
        nc.scalar.copy(out=blf[:], in_=tp[:, 4, 0:4])

        hpl = const.tile([P, 4, TOK], BF16)
        for j in range(4):
            hp = psum.tile([P, TOK], F32, tag="o", name="hp%d" % j)
            nc.tensor.matmul(hp[:], lhsT=wl[:, j * P:(j + 1) * P], rhs=xT[:], start=True, stop=True)
            nc.scalar.activation(out=hpl[:, j, :], in_=hp[:], func=ACT.Relu, bias=blf[:, j:j + 1], scale=1.0)

        def h_regroup(b):
            return regroup_views(hg[:, b, 1:3, :].rearrange("p e (q t) -> p (e q) t", t=4), hpl[:, :, b * N:(b + 1) * N])

        dst, src = h_regroup(1)
        nc.scalar.copy(out=dst, in_=src)
        alloc(0)
        copies_v(0, 0, NH)
        copies_s(0, 0, NH)
        load(RAW_UNITS)
        quant_w(0, 0, NH, (0, 1))
        dst, src = h_regroup(0)
        nc.vector.tensor_copy(out=dst, in_=src)
        nc.vector.tensor_copy(out=hg[:, :, 0, 4:4 * P], in_=hg[:, :, 2, 0:4 * P - 4])
        nc.vector.tensor_copy(out=hg[:, :, 3, 0:4 * P - 4], in_=hg[:, :, 1, 4:4 * P])
        hc = const.tile([P, B, 4, P], U32, align_bytes=64)
        hs = const.tile([P, B, 4, P], U8, align_bytes=64)
        for b in range(B):
            nc.vector.quantize_mx(
                out=hc[:, b, :, :].rearrange("p e q -> p (e q)").bitcast(FP8X4),
                scales=hs[:, b, :, :].rearrange("p e q -> p (e q)"),
                in_=hg[:, b, :, :].rearrange("p e x -> p (e x)"),
            )
        quant_w(0, 0, NH, (2,))

        tcq = const.tile([P, n_units, TOK], U32, align_bytes=64)
        tsq = const.tile([P, n_units, TOK], U8, align_bytes=64)
        gts = {}
        banks = {}

        def stage2(u, r, tts):
            wc, ws = wcs[u]
            if u not in gts:
                gts[u] = gtp.tile([P, 4, P, 4], BF16, align_bytes=64, tag="gt", name="gt_%d" % u)
            if (u, r) not in banks:
                banks[(u, r)] = psum.tile([P, 4, P], F32, tag="t", name="t_%d_%d" % (u, r))
            for tt in tts:
                for c in range(CTX):
                    cols = w_cols(u, c, tt)
                    nc.tensor.matmul_mx(
                        out=banks[(u, r)][:, tt, :],
                        lhsT=wc[:, cols].bitcast(FP8X4),
                        lhsT_scale=ws[:, cols],
                        rhs=hc[:, r // 2, r % 2 + c, :].bitcast(FP8X4),
                        rhs_scale=hs[:, r // 2, r % 2 + c, :],
                        start=(c == 0),
                        stop=(c == CTX - 1),
                    )

        def copy_t(u, r, engine):
            src = banks[(u, r)][:].rearrange("p t r -> p r t")
            if engine == "vector":
                nc.vector.tensor_copy(out=gts[u][:, r, :, :], in_=src)
            else:
                nc.scalar.copy(out=gts[u][:, r, :, :], in_=src)

        def quant_t(u, r0, r1):
            nc.vector.quantize_mx(
                out=tcq[:, u, r0 * P:r1 * P].bitcast(FP8X4),
                scales=tsq[:, u, r0 * P:r1 * P],
                in_=gts[u][:, r0:r1, :, :].rearrange("p r w t -> p (r w t)"),
            )

        blocks = [(b, ri, rj) for b in range(B) for ri in range(2) for rj in range(2)]
        obank = {}
        results = {}

        def stage3(k, us, tag):
            b, ri, rj = blocks[k]
            ti = (b * 2 + ri) * P
            if k not in obank:
                obank[k] = psum.tile([P, NO, P], F32, tag=tag, name="o_%d" % k)
            for u in us:
                o, g = units[u]
                nc.tensor.matmul_mx(
                    out=obank[k][:, o, :],
                    lhsT=tcq[:, u, ti:ti + P].bitcast(FP8X4),
                    lhsT_scale=tsq[:, u, ti:ti + P],
                    rhs=hc[:, b, rj + g, :].bitcast(FP8X4),
                    rhs_scale=hs[:, b, rj + g, :],
                    start=(g == 0),
                    stop=(g == CTX - 1),
                )

        def finish(k, cuts):
            b, ri, rj = blocks[k]
            if rj == 0:
                results[(b, ri)] = resp.tile([P, P, 2, NO], F32, tag="res", name="res_%d" % k)
            res = results[(b, ri)]
            for q0, q1 in zip(cuts, cuts[1:]):
                nc.vector.tensor_tensor(
                    out=res[:, q0:q1, rj, :],
                    in0=obank[k][:, :, q0:q1].rearrange("p o j -> p j o"),
                    in1=bb[:].unsqueeze(1).to_broadcast([P, q1 - q0, NO]),
                    op=ALU.add,
                )
                if rj == 1:
                    dst = out[b].rearrange("(q r) j o -> r q (j o)", r=2)[ri]
                    nc.sync.dma_start(
                        out=dst[:, q0 * 2 * NO:q1 * 2 * NO],
                        in_=res[:, q0:q1, :, :].rearrange("p q r o -> p (q r o)"),
                    )

        def early3(u):
            for k in range(4):
                stage3(k, [u], "o")

        for u in range(last - 1):
            alloc(u + 1)
            copies_v(u + 1, 0, NH)
            copies_s(u + 1, 0, NH)
            if u + 1 + RAW_UNITS < n_units:
                load(u + 1 + RAW_UNITS)
            if u >= 1:
                quant_t(u - 1, 0, 4)
            quant_w(u + 1, 0, NH, (0, 1))
            quant_w(u + 1, 0, NH, (2,))
            for r in range(4):
                stage2(u, r, range(4))
                copy_t(u, r, "scalar")
            if u >= 1:
                early3(u - 1)

        bb = const.tile([P, NO], BF16)
        nc.sync.dma_start(out=bb[:], in_=b_bil.partition_broadcast(P))

        u = last - 1
        alloc(last)
        for i, (g0, g1) in enumerate(LAST):
            copies_v(last, g0, g1)
            copies_s(last, g0, g1)
            if i == 0:
                quant_t(u - 1, 0, 4)
            if i >= 1:
                quant_w(last, LAST[i - 1][0], LAST[i - 1][1], (0, 1))
                quant_w(last, LAST[i - 1][0], LAST[i - 1][1], (2,))
            if i < 2:
                for r in (2 * i, 2 * i + 1):
                    stage2(u, r, range(4))
                    copy_t(u, r, "scalar")
        quant_w(last, LAST[-1][0], LAST[-1][1], (0, 1))
        quant_w(last, LAST[-1][0], LAST[-1][1], (2,))
        early3(u - 1)
        quant_t(u, 0, 4)
        for g0, g1 in LAST:
            for r in range(4):
                stage2(last, r, range(g0 // P, g1 // P))
        for r in range(4):
            copy_t(last, r, ("vector", "scalar")[r % 2])
        quant_t(last, 0, 2)
        quant_t(last, 2, 4)
        early3(u)
        stage3(4, range(last), "t")
        early3(last)
        for k in range(4):
            finish(k, (0, P))
        for k in range(5, 8):
            stage3(k - 1, [last], "t")
            stage3(k, range(last), "t")
            finish(k - 1, (0, P))
        stage3(7, [last], "t")
        finish(7, (0, P // 2, P))
